import numpy as np
import ml_dtypes


def mxq(x, axis, fmt="e4m3"):
    dtype, down = {"e4m3": (ml_dtypes.float8_e4m3fn, 7), "e5m2": (ml_dtypes.float8_e5m2, 14)}[fmt]
    v = np.moveaxis(np.asarray(x, np.float32).astype(ml_dtypes.bfloat16).astype(np.float64), axis, -1)
    blocks = v.reshape(v.shape[:-1] + (-1, 32))
    amax = np.abs(blocks).max(-1, keepdims=True)
    byte = np.maximum(np.where(amax > 0, np.frexp(amax)[1] - 1 + 127, 0) - down, 1)
    scale = np.exp2(byte - 127.0)
    codes = (blocks / scale).astype(np.float32).astype(dtype).astype(np.float64)
    return np.moveaxis((codes * scale).reshape(v.shape), -1, axis)


WIDE = False


def mx_kscale(k):
    if not WIDE:
        return np.ones(k)
    levels = np.array([10, -10, 5, -5, 0])
    a = np.random.permutation(np.resize(levels, k // 512 * 4)).reshape(k // 512, 4)
    idx = np.arange(k)
    return np.exp2(a[idx // 512, idx % 128 // 32])


BF16 = ml_dtypes.bfloat16


def bf(x):
    return np.asarray(x, np.float32).astype(BF16)


def f64(x):
    return np.asarray(x).astype(np.float64)


B, I, H, ORDER = 8192, 512, 256, 2
OH = ORDER * H


def sigmoid(v):
    return 1.0 / (1.0 + np.exp(-v))


def setup_inputs():
    s, t = mx_kscale(I), mx_kscale(OH)
    return {"x": bf(np.random.standard_normal((B, I)) * s),
            "me_output": bf(np.random.standard_normal((B, OH)) * t),
            "W_memi": bf(np.random.standard_normal((I, OH)) * 0.7 / np.sqrt(I) / s[:, None]),
            "W_memh": bf(np.random.standard_normal((OH, OH)) * 0.7 / np.sqrt(OH) / t[:, None]),
            "W_memt": bf(np.random.standard_normal((OH, H)) * 1.0 / np.sqrt(OH) / t[:, None]),
            "mem_bias": bf(np.random.standard_normal(OH) * 0.3)}


def reference(x, me_output, W_memi, W_memh, W_memt, mem_bias):
    me = f64(me_output)
    mg = ((mxq(f64(x), 1, "e4m3") @ mxq(f64(W_memi), 0, "e4m3"))
          + (mxq(me, 1, "e4m3") @ mxq(f64(W_memh), 0, "e4m3"))
          + f64(mem_bias))
    gated = sigmoid(mg) * me
    return mxq(gated, 1, "e4m3") @ mxq(f64(W_memt), 0, "e4m3")

@@ -1,0 +1,234 @@
+from contextlib import ExitStack
+
+import concourse.mybir as mybir
+from concourse.masks import make_identity
+
+F32 = mybir.dt.float32
+BF16 = mybir.dt.bfloat16
+U32 = mybir.dt.uint32
+U8 = mybir.dt.uint8
+FP8X4 = mybir.dt.float8_e4m3fn_x4
+ACT = mybir.ActivationFunctionType
+ALU = mybir.AluOpType
+
+B, I, OH, H = 8192, 512, 512, 256
+FLOPS = 2 * B * (I * OH + OH * OH + OH * H)
+
+P = 128
+BLK = 512
+NB = B // BLK
+R = BLK // P
+LOOKAHEAD = 6
+NAT_BUFS = 6
+
+
+def tile_lstmcell_pa_t_kernel(tc, x, me_output, W_memi, W_memh, W_memt, mem_bias, out):
+    nc = tc.nc
+    with ExitStack() as ctx:
+        consts = ctx.enter_context(tc.tile_pool(name="consts", bufs=1))
+        nat = ctx.enter_context(tc.tile_pool(name="nat", bufs=NAT_BUFS))
+        work = ctx.enter_context(tc.tile_pool(name="work", bufs=2))
+        psum = ctx.enter_context(tc.psum_pool(name="psum", bufs=1))
+        ctx.enter_context(tc.manual_schedule())
+
+        counter = [0]
+
+        def new_bank():
+            n = counter[0]
+            counter[0] = n + 1
+            return psum.tile([P, 512], F32, name="ps%d" % n, tag="bank%d" % (n % 8))
+
+        st = {}
+
+        warm = consts.tile([P, 1], F32, name="warm")
+        nc.vector.memset(warm[:], 0.0)
+        nc.scalar.activation(out=warm[:], in_=warm[:], func=ACT.Sigmoid)
+
+        ident = consts.tile([P, P], F32, name="ident")
+        make_identity(nc, ident[:])
+
+        bias_raw = consts.tile([P, 4], BF16, name="bias_raw")
+        with nc.allow_non_contiguous_dma(reason="512 bias values, two to a piece"):
+            nc.scalar.dma_start(
+                out=bias_raw[:].rearrange("p (u e) -> p u e", u=2),
+                in_=mem_bias.rearrange("(u p e) -> p u e", u=2, e=2),
+            )
+
+        def load_w(w, cols, nm):
+            raw = consts.tile([P, 4 * cols], BF16, name=nm + "_raw")
+            nc.sync.dma_start(
+                out=raw[:].rearrange("p (u f) -> p u f", u=2),
+                in_=w.rearrange("(u p e) c -> p u (e c)", u=2, e=2),
+            )
+            return raw
+
+        def load(j):
+            rows = slice(j * BLK, (j + 1) * BLK)
+            xn = nat.tile([P, R * I], BF16, name="xn%d" % j, tag="xn")
+            nc.sync.dma_start(out=xn[:], in_=x[rows, :].rearrange("(p r) k -> p (r k)", r=R))
+            en = nat.tile([P, R * OH], BF16, name="en%d" % j, tag="en")
+            nc.sync.dma_start(out=en[:], in_=me_output[rows, :].rearrange("(p r) k -> p (r k)", r=R))
+            st[("xn", j)] = xn
+            st[("en", j)] = en
+
+        wi_raw = load_w(W_memi, OH, "wi")
+        wh_raw = load_w(W_memh, OH, "wh")
+        load(0)
+        load(1)
+        wt_raw = load_w(W_memt, H, "wt")
+        load(2)
+        load(3)
+
+        bias_f = consts.tile([P, 4], F32, name="bias_f")
+        nc.vector.tensor_copy(out=bias_f[:], in_=bias_raw[:])
+
+        def regroup_gate_w(raw, nm, engines):
+            grp = consts.tile([P, 4 * OH], BF16, name=nm + "_grp", align_bytes=64)
+            src = raw[:].rearrange("p (t u q e) -> p u e q t", t=4, u=2, e=2)
+            for m in range(4):
+                dst = grp[:, m * 512:(m + 1) * 512].rearrange("p (q t) -> p q t", t=4)
+                if engines[m] == "v":
+                    nc.vector.tensor_copy(out=dst, in_=src[:, m // 2, m % 2])
+                else:
+                    nc.scalar.copy(out=dst, in_=src[:, m // 2, m % 2])
+            return grp
+
+        def quant_w(grp, cols, nm):
+            codes = consts.tile([P, cols], U32, name=nm + "_codes", align_bytes=64)
+            scales = consts.tile([P, cols], U8, name=nm + "_scales", align_bytes=64)
+            nc.vector.quantize_mx(out=codes[:].bitcast(FP8X4), scales=scales[:], in_=grp[:])
+            return codes, scales
+
+        wi_grp = regroup_gate_w(wi_raw, "wi", "vvvv")
+        wh_grp = regroup_gate_w(wh_raw, "wh", "ssvv")
+        wic, wis = quant_w(wi_grp, OH, "wi")
+        whc, whs = quant_w(wh_grp, OH, "wh")
+
+        def prep_wt():
+            grp = consts.tile([P, 4 * H], BF16, name="wt_grp", align_bytes=64)
+            nc.vector.tensor_copy(
+                out=grp[:].rearrange("p (h t) -> p h t", t=4),
+                in_=wt_raw[:].rearrange("p (t h) -> p h t", t=4),
+            )
+            st["wt_grp"] = grp
+
+        def quant_wt():
+            st["wt"] = quant_w(st["wt_grp"], H, "wt")
+
+        def transposes(j):
+            for key in ("xn", "en"):
+                words = st[(key, j)][:].bitcast(F32)
+                for h in range(2):
+                    bank = new_bank()
+                    for rr in range(2):
+                        for u in range(2):
+                            c0 = (2 * h + rr) * 256 + u * P
+                            nc.tensor.transpose(
+                                bank[:, u * 256 + rr * P:u * 256 + (rr + 1) * P],
+                                words[:, c0:c0 + P],
+                                ident[:],
+                            )
+                    st[("T", key, j, h)] = bank
+
+        def exits(j):
+            gx = work.tile([P, 4 * BLK], BF16, name="gx%d" % j, tag="gx", align_bytes=64)
+            ge = work.tile([P, 4 * BLK], BF16, name="ge%d" % j, tag="ge", bufs=3, align_bytes=64)
+            st[("gx", j)] = gx
+            st[("ge", j)] = ge
+            n_vec = 2 if j % 2 else 1
+            plan = [("xn", gx, 0), ("xn", gx, 1), ("en", ge, 0), ("en", ge, 1)]
+            for i, (key, dst, h) in enumerate(plan):
+                src = st[("T", key, j, h)][:].rearrange("q (u c) -> q c u", u=2)
+                d = dst[:].bitcast(F32)[:, h * 512:(h + 1) * 512].rearrange("q (c u) -> q c u", u=2)
+                if i >= 4 - n_vec:
+                    nc.vector.tensor_copy(out=d, in_=src)
+                else:
+                    nc.scalar.copy(out=d, in_=src)
+
+        def quant(src, nm, j):
+            codes = work.tile([P, BLK], U32, name="%sc%d" % (nm, j), tag=nm + "c", align_bytes=64)
+            scales = work.tile([P, BLK], U8, name="%ss%d" % (nm, j), tag=nm + "s", align_bytes=64)
+            nc.vector.quantize_mx(out=codes[:].bitcast(FP8X4), scales=scales[:], in_=src[:])
+            st[(nm, j)] = (codes, scales)
+
+        def stage1(j):
+            xc, xs = st[("x", j)]
+            ec, es = st[("e", j)]
+            for m in range(4):
+                cols = slice(m * P, (m + 1) * P)
+                bank = new_bank()
+                nc.tensor.matmul_mx(
+                    out=bank[:], lhsT=wic[:, cols].bitcast(FP8X4), lhsT_scale=wis[:, cols],
+                    rhs=xc[:].bitcast(FP8X4), rhs_scale=xs[:], start=True, stop=False,
+                )
+                nc.tensor.matmul_mx(
+                    out=bank[:], lhsT=whc[:, cols].bitcast(FP8X4), lhsT_scale=whs[:, cols],
+                    rhs=ec[:].bitcast(FP8X4), rhs_scale=es[:], start=False, stop=True,
+                )
+                st[("M", j, m)] = bank
+
+        def sigmoid(j):
+            sig = work.tile([P, 4 * BLK], F32, name="sig%d" % j, tag="sig")
+            for m in range(4):
+                nc.scalar.activation(
+                    out=sig[:, m * BLK:(m + 1) * BLK], in_=st[("M", j, m)][:],
+                    func=ACT.Sigmoid, bias=bias_f[:, m:m + 1], scale=1.0,
+                )
+            st[("sig", j)] = sig
+
+        def mult(j):
+            gg = work.tile([P, 4 * BLK], BF16, name="gg%d" % j, tag="gg", align_bytes=64)
+            nc.vector.tensor_tensor(
+                out=gg[:].rearrange("p (c t) -> p c t", t=4),
+                in0=st[("sig", j)][:].rearrange("p (t c) -> p c t", t=4),
+                in1=st[("ge", j)][:].rearrange("p (c t) -> p c t", t=4),
+                op=ALU.mult,
+            )
+            st[("gg", j)] = gg
+
+        def stage2(j):
+            gc, gs = st[("g", j)]
+            wtc, wts = st["wt"]
+            for h in range(2):
+                bank = new_bank()
+                for rr in range(2):
+                    cols = slice((2 * h + rr) * P, (2 * h + rr + 1) * P)
+                    nc.tensor.matmul_mx(
+                        out=bank[:, rr * H:(rr + 1) * H],
+                        lhsT=gc[:, cols].bitcast(FP8X4), lhsT_scale=gs[:, cols],
+                        rhs=wtc[:].bitcast(FP8X4), rhs_scale=wts[:], start=True, stop=True,
+                    )
+                st[("O", j, h)] = bank
+
+        def oexit_store(j):
+            osb = work.tile([P, R * H], F32, name="osb%d" % j, tag="osb", bufs=3)
+            for h in range(2):
+                nc.scalar.copy(out=osb[:, h * 512:(h + 1) * 512], in_=st[("O", j, h)][:])
+            nc.sync.dma_start(
+                out=out[j * BLK:(j + 1) * BLK, :].rearrange("(p r) h -> p (r h)", r=R), in_=osb[:]
+            )
+
+        for j in range(-2, NB):
+            if 4 <= j + LOOKAHEAD < NB:
+                load(j + LOOKAHEAD)
+            if j + 2 < NB:
+                transposes(j + 2)
+            if j >= 0:
+                mult(j)
+            if j + 2 < NB:
+                exits(j + 2)
+            if j == -1:
+                prep_wt()
+            if j >= 0:
+                quant(st[("gg", j)], "g", j)
+            if 0 <= j + 1 < NB:
+                stage1(j + 1)
+                sigmoid(j + 1)
+            if j + 2 < NB:
+                quant(st[("gx", j + 2)], "x", j + 2)
+                quant(st[("ge", j + 2)], "e", j + 2)
+            if j == -1:
+                quant_wt()
+            if j >= 0:
+                stage2(j)
+                oexit_store(j)

@@ -179,9 +179,9 @@ def tile_lstmcell_pa_t_kernel(tc, x, me_output, W_memi, W_memh, W_memt, mem_bias
         def mult(j):
             gg = work.tile([P, 4 * BLK], BF16, name="gg%d" % j, tag="gg", align_bytes=64)
             nc.vector.tensor_tensor(
-                out=gg[:].rearrange("p (c t) -> p c t", t=4),
-                in0=st[("sig", j)][:].rearrange("p (t c) -> p c t", t=4),
-                in1=st[("ge", j)][:].rearrange("p (c t) -> p c t", t=4),
+                out=gg[:].rearrange("p (c i t) -> p c t i", i=4, t=4),
+                in0=st[("sig", j)][:].rearrange("p (t c i) -> p c t i", t=4, i=4),
+                in1=st[("ge", j)][:].rearrange("p (c i t) -> p c t i", i=4, t=4),
                 op=ALU.mult,
             )
             st[("gg", j)] = gg

@@ -15,11 +15,13 @@ B, I, OH, H = 8192, 512, 512, 256
 FLOPS = 2 * B * (I * OH + OH * OH + OH * H)
 
 P = 128
-BLK = 512
-NB = B // BLK
-R = BLK // P
+ROW_TILES = [2, 2] + [4] * 14 + [2, 2]
+NB = len(ROW_TILES)
+ROW0 = [P * sum(ROW_TILES[:j]) for j in range(NB)]
+assert P * sum(ROW_TILES) == B
 LOOKAHEAD = 6
 NAT_BUFS = 6
+S2_LAG = 1
 
 
 def tile_lstmcell_pa_t_kernel(tc, x, me_output, W_memi, W_memh, W_memt, mem_bias, out):
@@ -63,11 +65,12 @@ def tile_lstmcell_pa_t_kernel(tc, x, me_output, W_memi, W_memh, W_memt, mem_bias
             return raw
 
         def load(j):
-            rows = slice(j * BLK, (j + 1) * BLK)
-            xn = nat.tile([P, R * I], BF16, name="xn%d" % j, tag="xn")
-            nc.sync.dma_start(out=xn[:], in_=x[rows, :].rearrange("(p r) k -> p (r k)", r=R))
-            en = nat.tile([P, R * OH], BF16, name="en%d" % j, tag="en")
-            nc.sync.dma_start(out=en[:], in_=me_output[rows, :].rearrange("(p r) k -> p (r k)", r=R))
+            nr = ROW_TILES[j]
+            rows = slice(ROW0[j], ROW0[j] + nr * P)
+            xn = nat.tile([P, nr * I], BF16, name="xn%d" % j, tag="xn")
+            nc.sync.dma_start(out=xn[:], in_=x[rows, :].rearrange("(p r) k -> p (r k)", r=nr))
+            en = nat.tile([P, nr * OH], BF16, name="en%d" % j, tag="en")
+            nc.sync.dma_start(out=en[:], in_=me_output[rows, :].rearrange("(p r) k -> p (r k)", r=nr))
             st[("xn", j)] = xn
             st[("en", j)] = en
 
@@ -78,6 +81,7 @@ def tile_lstmcell_pa_t_kernel(tc, x, me_output, W_memi, W_memh, W_memt, mem_bias
         wt_raw = load_w(W_memt, H, "wt")
         load(2)
         load(3)
+        loaded = [4]
 
         bias_f = consts.tile([P, 4], F32, name="bias_f")
         nc.vector.tensor_copy(out=bias_f[:], in_=bias_raw[:])
@@ -118,7 +122,7 @@ def tile_lstmcell_pa_t_kernel(tc, x, me_output, W_memi, W_memh, W_memt, mem_bias
         def transposes(j):
             for key in ("xn", "en"):
                 words = st[(key, j)][:].bitcast(F32)
-                for h in range(2):
+                for h in range(ROW_TILES[j] // 2):
                     bank = new_bank()
                     for rr in range(2):
                         for u in range(2):
@@ -131,53 +135,62 @@ def tile_lstmcell_pa_t_kernel(tc, x, me_output, W_memi, W_memh, W_memt, mem_bias
                     st[("T", key, j, h)] = bank
 
         def exits(j):
-            gx = work.tile([P, 4 * BLK], BF16, name="gx%d" % j, tag="gx", align_bytes=64)
-            ge = work.tile([P, 4 * BLK], BF16, name="ge%d" % j, tag="ge", bufs=3, align_bytes=64)
+            nr = ROW_TILES[j]
+            gx = work.tile([P, nr * 512], BF16, name="gx%d" % j, tag="gx", align_bytes=64)
+            ge = work.tile([P, nr * 512], BF16, name="ge%d" % j, tag="ge", bufs=3, align_bytes=64)
             st[("gx", j)] = gx
             st[("ge", j)] = ge
-            n_vec = 2 if j % 2 else 1
-            plan = [("xn", gx, 0), ("xn", gx, 1), ("en", ge, 0), ("en", ge, 1)]
+            plan = [("xn", gx, h) for h in range(nr // 2)] + [("en", ge, h) for h in range(nr // 2)]
+            n_vec = 1 if (nr == 2 or j % 2 == 0) else 2
             for i, (key, dst, h) in enumerate(plan):
                 src = st[("T", key, j, h)][:].rearrange("q (u c) -> q c u", u=2)
                 d = dst[:].bitcast(F32)[:, h * 512:(h + 1) * 512].rearrange("q (c u) -> q c u", u=2)
-                if i >= 4 - n_vec:
+                if i >= len(plan) - n_vec:
                     nc.vector.tensor_copy(out=d, in_=src)
                 else:
                     nc.scalar.copy(out=d, in_=src)
 
-        def quant(src, nm, j):
-            codes = work.tile([P, BLK], U32, name="%sc%d" % (nm, j), tag=nm + "c", align_bytes=64)
-            scales = work.tile([P, BLK], U8, name="%ss%d" % (nm, j), tag=nm + "s", align_bytes=64)
+        def quant(src, nm, j, bufs):
+            cols = ROW_TILES[j] * P
+            codes = work.tile([P, cols], U32, name="%sc%d" % (nm, j), tag=nm + "c", bufs=bufs, align_bytes=64)
+            scales = work.tile([P, cols], U8, name="%ss%d" % (nm, j), tag=nm + "s", bufs=bufs, align_bytes=64)
             nc.vector.quantize_mx(out=codes[:].bitcast(FP8X4), scales=scales[:], in_=src[:])
             st[(nm, j)] = (codes, scales)
 
         def stage1(j):
+            n = ROW_TILES[j] * P
+            per_bank = 512 // n
             xc, xs = st[("x", j)]
             ec, es = st[("e", j)]
+            bank = None
             for m in range(4):
                 cols = slice(m * P, (m + 1) * P)
-                bank = new_bank()
+                if m % per_bank == 0:
+                    bank = new_bank()
+                acc = bank[:, (m % per_bank) * n:(m % per_bank + 1) * n]
                 nc.tensor.matmul_mx(
-                    out=bank[:], lhsT=wic[:, cols].bitcast(FP8X4), lhsT_scale=wis[:, cols],
+                    out=acc, lhsT=wic[:, cols].bitcast(FP8X4), lhsT_scale=wis[:, cols],
                     rhs=xc[:].bitcast(FP8X4), rhs_scale=xs[:], start=True, stop=False,
                 )
                 nc.tensor.matmul_mx(
-                    out=bank[:], lhsT=whc[:, cols].bitcast(FP8X4), lhsT_scale=whs[:, cols],
+                    out=acc, lhsT=whc[:, cols].bitcast(FP8X4), lhsT_scale=whs[:, cols],
                     rhs=ec[:].bitcast(FP8X4), rhs_scale=es[:], start=False, stop=True,
                 )
-                st[("M", j, m)] = bank
+                st[("M", j, m)] = acc
 
         def sigmoid(j):
-            sig = work.tile([P, 4 * BLK], F32, name="sig%d" % j, tag="sig")
+            n = ROW_TILES[j] * P
+            sig = work.tile([P, 4 * n], F32, name="sig%d" % j, tag="sig")
             for m in range(4):
                 nc.scalar.activation(
-                    out=sig[:, m * BLK:(m + 1) * BLK], in_=st[("M", j, m)][:],
+                    out=sig[:, m * n:(m + 1) * n], in_=st[("M", j, m)],
                     func=ACT.Sigmoid, bias=bias_f[:, m:m + 1], scale=1.0,
                 )
             st[("sig", j)] = sig
 
         def mult(j):
-            gg = work.tile([P, 4 * BLK], BF16, name="gg%d" % j, tag="gg", align_bytes=64)
+            n = ROW_TILES[j] * P
+            gg = work.tile([P, 4 * n], BF16, name="gg%d" % j, tag="gg", align_bytes=64)
             nc.vector.tensor_tensor(
                 out=gg[:].rearrange("p (c i t) -> p c t i", i=4, t=4),
                 in0=st[("sig", j)][:].rearrange("p (t c i) -> p c t i", t=4, i=4),
@@ -189,7 +202,7 @@ def tile_lstmcell_pa_t_kernel(tc, x, me_output, W_memi, W_memh, W_memt, mem_bias
         def stage2(j):
             gc, gs = st[("g", j)]
             wtc, wts = st["wt"]
-            for h in range(2):
+            for h in range(ROW_TILES[j] // 2):
                 bank = new_bank()
                 for rr in range(2):
                     cols = slice((2 * h + rr) * P, (2 * h + rr + 1) * P)
@@ -201,34 +214,36 @@ def tile_lstmcell_pa_t_kernel(tc, x, me_output, W_memi, W_memh, W_memt, mem_bias
                 st[("O", j, h)] = bank
 
         def oexit_store(j):
-            osb = work.tile([P, R * H], F32, name="osb%d" % j, tag="osb", bufs=3)
-            for h in range(2):
+            nr = ROW_TILES[j]
+            osb = work.tile([P, nr * H], F32, name="osb%d" % j, tag="osb", bufs=3)
+            for h in range(nr // 2):
                 nc.scalar.copy(out=osb[:, h * 512:(h + 1) * 512], in_=st[("O", j, h)][:])
             nc.sync.dma_start(
-                out=out[j * BLK:(j + 1) * BLK, :].rearrange("(p r) h -> p (r h)", r=R), in_=osb[:]
+                out=out[ROW0[j]:ROW0[j] + nr * P, :].rearrange("(p r) h -> p (r h)", r=nr), in_=osb[:]
             )
 
-        for j in range(-2, NB):
-            if 4 <= j + LOOKAHEAD < NB:
-                load(j + LOOKAHEAD)
-            if j + 2 < NB:
-                transposes(j + 2)
-            if j >= 0:
-                mult(j)
-            if j + 2 < NB:
-                exits(j + 2)
-            if j == -1:
+        for s in range(-2, NB + S2_LAG):
+            while loaded[0] < NB and loaded[0] <= s + LOOKAHEAD:
+                load(loaded[0])
+                loaded[0] += 1
+            if s + 2 < NB:
+                transposes(s + 2)
+            if 0 <= s < NB:
+                mult(s)
+            if s + 2 < NB:
+                exits(s + 2)
+            if s == -1:
                 prep_wt()
-            if j >= 0:
-                quant(st[("gg", j)], "g", j)
-            if 0 <= j + 1 < NB:
-                stage1(j + 1)
-                sigmoid(j + 1)
-            if j + 2 < NB:
-                quant(st[("gx", j + 2)], "x", j + 2)
-                quant(st[("ge", j + 2)], "e", j + 2)
-            if j == -1:
+            if 0 <= s < NB:
+                quant(st[("gg", s)], "g", s, 2 + S2_LAG)
+            if 0 <= s + 1 < NB:
+                stage1(s + 1)
+                sigmoid(s + 1)
+            if s + 2 < NB:
+                quant(st[("gx", s + 2)], "x", s + 2, 2)
+                quant(st[("ge", s + 2)], "e", s + 2, 2)
+            if s == -1:
                 quant_wt()
-            if j >= 0:
-                stage2(j)
-                oexit_store(j)
+            if 0 <= s - S2_LAG < NB:
+                stage2(s - S2_LAG)
+                oexit_store(s - S2_LAG)

@@ -141,7 +141,7 @@ def tile_lstmcell_pa_t_kernel(tc, x, me_output, W_memi, W_memh, W_memt, mem_bias
             st[("gx", j)] = gx
             st[("ge", j)] = ge
             plan = [("xn", gx, h) for h in range(nr // 2)] + [("en", ge, h) for h in range(nr // 2)]
-            n_vec = 1 if (nr == 2 or j % 2 == 0) else 2
+            n_vec = 1
             for i, (key, dst, h) in enumerate(plan):
                 src = st[("T", key, j, h)][:].rearrange("q (u c) -> q c u", u=2)
                 d = dst[:].bitcast(F32)[:, h * 512:(h + 1) * 512].rearrange("q (c u) -> q c u", u=2)

@@ -24,6 +24,16 @@ NAT_BUFS = 6
 S2_LAG = 1
 
 
+def vector_exits(j):
+    return 2 if ROW_TILES[j] == 4 and j % 2 == 1 else 1
+
+
+def gpsimd_cols(j):
+    if ROW_TILES[j] != 4:
+        return 0
+    return 96 if vector_exits(j + 2) == 2 else 48
+
+
 def tile_lstmcell_pa_t_kernel(tc, x, me_output, W_memi, W_memh, W_memt, mem_bias, out):
     nc = tc.nc
     with ExitStack() as ctx:
@@ -141,7 +151,7 @@ def tile_lstmcell_pa_t_kernel(tc, x, me_output, W_memi, W_memh, W_memt, mem_bias
             st[("gx", j)] = gx
             st[("ge", j)] = ge
             plan = [("xn", gx, h) for h in range(nr // 2)] + [("en", ge, h) for h in range(nr // 2)]
-            n_vec = 1
+            n_vec = vector_exits(j)
             for i, (key, dst, h) in enumerate(plan):
                 src = st[("T", key, j, h)][:].rearrange("q (u c) -> q c u", u=2)
                 d = dst[:].bitcast(F32)[:, h * 512:(h + 1) * 512].rearrange("q (c u) -> q c u", u=2)
@@ -191,12 +201,22 @@ def tile_lstmcell_pa_t_kernel(tc, x, me_output, W_memi, W_memh, W_memt, mem_bias
         def mult(j):
             n = ROW_TILES[j] * P
             gg = work.tile([P, 4 * n], BF16, name="gg%d" % j, tag="gg", align_bytes=64)
+            nv = n - gpsimd_cols(j)
+            planes = st[("sig", j)][:].rearrange("p (t c) -> p t c", t=4)
+            ge = st[("ge", j)]
             nc.vector.tensor_tensor(
-                out=gg[:].rearrange("p (c i t) -> p c t i", i=4, t=4),
-                in0=st[("sig", j)][:].rearrange("p (t c i) -> p c t i", t=4, i=4),
-                in1=st[("ge", j)][:].rearrange("p (c i t) -> p c t i", i=4, t=4),
+                out=gg[:, :4 * nv].rearrange("p (c i t) -> p c t i", i=4, t=4),
+                in0=planes[:, :, :nv].rearrange("p t (c i) -> p c t i", i=4),
+                in1=ge[:, :4 * nv].rearrange("p (c i t) -> p c t i", i=4, t=4),
                 op=ALU.mult,
             )
+            if nv < n:
+                nc.gpsimd.tensor_tensor(
+                    out=gg[:, 4 * nv:].rearrange("p (c t) -> p c t", t=4),
+                    in0=planes[:, :, nv:].rearrange("p t c -> p c t"),
+                    in1=ge[:, 4 * nv:].rearrange("p (c t) -> p c t", t=4),
+                    op=ALU.mult,
+                )
             st[("gg", j)] = gg
 
         def stage2(j):
@@ -234,14 +254,14 @@ def tile_lstmcell_pa_t_kernel(tc, x, me_output, W_memi, W_memh, W_memt, mem_bias
                 exits(s + 2)
             if s == -1:
                 prep_wt()
-            if 0 <= s < NB:
-                quant(st[("gg", s)], "g", s, 2 + S2_LAG)
             if 0 <= s + 1 < NB:
                 stage1(s + 1)
                 sigmoid(s + 1)
             if s + 2 < NB:
                 quant(st[("gx", s + 2)], "x", s + 2, 2)
                 quant(st[("ge", s + 2)], "e", s + 2, 2)
+            if 0 <= s < NB:
+                quant(st[("gg", s)], "g", s, 2 + S2_LAG)
             if s == -1:
                 quant_wt()
             if 0 <= s - S2_LAG < NB:

@@ -25,11 +25,13 @@ S2_LAG = 1
 
 
 def vector_exits(j):
+    if j < 2:
+        return 0
     return 2 if ROW_TILES[j] == 4 and j % 2 == 1 else 1
 
 
 def gpsimd_cols(j):
-    if ROW_TILES[j] != 4:
+    if ROW_TILES[j] != 4 or j + 2 >= NB:
         return 0
     return 96 if vector_exits(j + 2) == 2 else 48
 
@@ -93,9 +95,6 @@ def tile_lstmcell_pa_t_kernel(tc, x, me_output, W_memi, W_memh, W_memt, mem_bias
         load(3)
         loaded = [4]
 
-        bias_f = consts.tile([P, 4], F32, name="bias_f")
-        nc.vector.tensor_copy(out=bias_f[:], in_=bias_raw[:])
-
         def regroup_gate_w(raw, nm, engines):
             grp = consts.tile([P, 4 * OH], BF16, name=nm + "_grp", align_bytes=64)
             src = raw[:].rearrange("p (t u q e) -> p u e q t", t=4, u=2, e=2)
@@ -113,14 +112,16 @@ def tile_lstmcell_pa_t_kernel(tc, x, me_output, W_memi, W_memh, W_memt, mem_bias
             nc.vector.quantize_mx(out=codes[:].bitcast(FP8X4), scales=scales[:], in_=grp[:])
             return codes, scales
 
-        wi_grp = regroup_gate_w(wi_raw, "wi", "vvvv")
-        wh_grp = regroup_gate_w(wh_raw, "wh", "ssvv")
+        wi_grp = regroup_gate_w(wi_raw, "wi", "vvvs")
         wic, wis = quant_w(wi_grp, OH, "wi")
+        wh_grp = regroup_gate_w(wh_raw, "wh", "ssvv")
         whc, whs = quant_w(wh_grp, OH, "wh")
+        bias_f = consts.tile([P, 4], F32, name="bias_f")
+        nc.vector.tensor_copy(out=bias_f[:], in_=bias_raw[:])
 
         def prep_wt():
             grp = consts.tile([P, 4 * H], BF16, name="wt_grp", align_bytes=64)
-            nc.vector.tensor_copy(
+            nc.scalar.copy(
                 out=grp[:].rearrange("p (h t) -> p h t", t=4),
                 in_=wt_raw[:].rearrange("p (t h) -> p h t", t=4),
             )

@@ -27,7 +27,7 @@ S2_LAG = 1
 def vector_exits(j):
     if j < 2:
         return 0
-    return 2 if ROW_TILES[j] == 4 and j % 2 == 1 else 1
+    return 2 if ROW_TILES[j] == 4 and j % 3 == 1 else 1
 
 
 def gpsimd_cols(j):
@@ -121,7 +121,7 @@ def tile_lstmcell_pa_t_kernel(tc, x, me_output, W_memi, W_memh, W_memt, mem_bias
 
         def prep_wt():
             grp = consts.tile([P, 4 * H], BF16, name="wt_grp", align_bytes=64)
-            nc.scalar.copy(
+            nc.vector.tensor_copy(
                 out=grp[:].rearrange("p (h t) -> p h t", t=4),
                 in_=wt_raw[:].rearrange("p (t h) -> p h t", t=4),
             )
@@ -253,8 +253,8 @@ def tile_lstmcell_pa_t_kernel(tc, x, me_output, W_memi, W_memh, W_memt, mem_bias
                 mult(s)
             if s + 2 < NB:
                 exits(s + 2)
-            if s == -1:
-                prep_wt()
+            if s == 0:
+                quant_wt()
             if 0 <= s + 1 < NB:
                 stage1(s + 1)
                 sigmoid(s + 1)
@@ -264,7 +264,7 @@ def tile_lstmcell_pa_t_kernel(tc, x, me_output, W_memi, W_memh, W_memt, mem_bias
             if 0 <= s < NB:
                 quant(st[("gg", s)], "g", s, 2 + S2_LAG)
             if s == -1:
-                quant_wt()
+                prep_wt()
             if 0 <= s - S2_LAG < NB:
                 stage2(s - S2_LAG)
                 oexit_store(s - S2_LAG)

@@ -33,7 +33,7 @@ def vector_exits(j):
 def gpsimd_cols(j):
     if ROW_TILES[j] != 4 or j + 2 >= NB:
         return 0
-    return 96 if vector_exits(j + 2) == 2 else 48
+    return 128 if vector_exits(j + 2) == 2 else 64
 
 
 def tile_lstmcell_pa_t_kernel(tc, x, me_output, W_memi, W_memh, W_memt, mem_bias, out):

from contextlib import ExitStack

import concourse.mybir as mybir
from concourse.masks import make_identity

F32 = mybir.dt.float32
BF16 = mybir.dt.bfloat16
U32 = mybir.dt.uint32
U8 = mybir.dt.uint8
FP8X4 = mybir.dt.float8_e4m3fn_x4
ACT = mybir.ActivationFunctionType
ALU = mybir.AluOpType

B, I, OH, H = 8192, 512, 512, 256
FLOPS = 2 * B * (I * OH + OH * OH + OH * H)

P = 128
ROW_TILES = [2, 2] + [4] * 14 + [2, 2]
NB = len(ROW_TILES)
ROW0 = [P * sum(ROW_TILES[:j]) for j in range(NB)]
assert P * sum(ROW_TILES) == B
LOOKAHEAD = 6
NAT_BUFS = 6
S2_LAG = 1


def vector_exits(j):
    if j < 2:
        return 0
    return 2 if ROW_TILES[j] == 4 and j % 3 == 1 else 1


def gpsimd_cols(j):
    if ROW_TILES[j] != 4 or j + 2 >= NB:
        return 0
    return 128 if vector_exits(j + 2) == 2 else 64


def tile_lstmcell_pa_t_kernel(tc, x, me_output, W_memi, W_memh, W_memt, mem_bias, out):
    nc = tc.nc
    with ExitStack() as ctx:
        consts = ctx.enter_context(tc.tile_pool(name="consts", bufs=1))
        nat = ctx.enter_context(tc.tile_pool(name="nat", bufs=NAT_BUFS))
        work = ctx.enter_context(tc.tile_pool(name="work", bufs=2))
        psum = ctx.enter_context(tc.psum_pool(name="psum", bufs=1))
        ctx.enter_context(tc.manual_schedule())

        counter = [0]

        def new_bank():
            n = counter[0]
            counter[0] = n + 1
            return psum.tile([P, 512], F32, name="ps%d" % n, tag="bank%d" % (n % 8))

        st = {}

        warm = consts.tile([P, 1], F32, name="warm")
        nc.vector.memset(warm[:], 0.0)
        nc.scalar.activation(out=warm[:], in_=warm[:], func=ACT.Sigmoid)

        ident = consts.tile([P, P], F32, name="ident")
        make_identity(nc, ident[:])

        bias_raw = consts.tile([P, 4], BF16, name="bias_raw")
        with nc.allow_non_contiguous_dma(reason="512 bias values, two to a piece"):
            nc.scalar.dma_start(
                out=bias_raw[:].rearrange("p (u e) -> p u e", u=2),
                in_=mem_bias.rearrange("(u p e) -> p u e", u=2, e=2),
            )

        def load_w(w, cols, nm):
            raw = consts.tile([P, 4 * cols], BF16, name=nm + "_raw")
            nc.sync.dma_start(
                out=raw[:].rearrange("p (u f) -> p u f", u=2),
                in_=w.rearrange("(u p e) c -> p u (e c)", u=2, e=2),
            )
            return raw

        def load(j):
            nr = ROW_TILES[j]
            rows = slice(ROW0[j], ROW0[j] + nr * P)
            xn = nat.tile([P, nr * I], BF16, name="xn%d" % j, tag="xn")
            nc.sync.dma_start(out=xn[:], in_=x[rows, :].rearrange("(p r) k -> p (r k)", r=nr))
            en = nat.tile([P, nr * OH], BF16, name="en%d" % j, tag="en")
            nc.sync.dma_start(out=en[:], in_=me_output[rows, :].rearrange("(p r) k -> p (r k)", r=nr))
            st[("xn", j)] = xn
            st[("en", j)] = en

        wi_raw = load_w(W_memi, OH, "wi")
        wh_raw = load_w(W_memh, OH, "wh")
        load(0)
        load(1)
        wt_raw = load_w(W_memt, H, "wt")
        load(2)
        load(3)
        loaded = [4]

        def regroup_gate_w(raw, nm, engines):
            grp = consts.tile([P, 4 * OH], BF16, name=nm + "_grp", align_bytes=64)
            src = raw[:].rearrange("p (t u q e) -> p u e q t", t=4, u=2, e=2)
            for m in range(4):
                dst = grp[:, m * 512:(m + 1) * 512].rearrange("p (q t) -> p q t", t=4)
                if engines[m] == "v":
                    nc.vector.tensor_copy(out=dst, in_=src[:, m // 2, m % 2])
                else:
                    nc.scalar.copy(out=dst, in_=src[:, m // 2, m % 2])
            return grp

        def quant_w(grp, cols, nm):
            codes = consts.tile([P, cols], U32, name=nm + "_codes", align_bytes=64)
            scales = consts.tile([P, cols], U8, name=nm + "_scales", align_bytes=64)
            nc.vector.quantize_mx(out=codes[:].bitcast(FP8X4), scales=scales[:], in_=grp[:])
            return codes, scales

        wi_grp = regroup_gate_w(wi_raw, "wi", "vvvs")
        wic, wis = quant_w(wi_grp, OH, "wi")
        wh_grp = regroup_gate_w(wh_raw, "wh", "ssvv")
        whc, whs = quant_w(wh_grp, OH, "wh")
        bias_f = consts.tile([P, 4], F32, name="bias_f")
        nc.vector.tensor_copy(out=bias_f[:], in_=bias_raw[:])

        def prep_wt():
            grp = consts.tile([P, 4 * H], BF16, name="wt_grp", align_bytes=64)
            nc.vector.tensor_copy(
                out=grp[:].rearrange("p (h t) -> p h t", t=4),
                in_=wt_raw[:].rearrange("p (t h) -> p h t", t=4),
            )
            st["wt_grp"] = grp

        def quant_wt():
            st["wt"] = quant_w(st["wt_grp"], H, "wt")

        def transposes(j):
            for key in ("xn", "en"):
                words = st[(key, j)][:].bitcast(F32)
                for h in range(ROW_TILES[j] // 2):
                    bank = new_bank()
                    for rr in range(2):
                        for u in range(2):
                            c0 = (2 * h + rr) * 256 + u * P
                            nc.tensor.transpose(
                                bank[:, u * 256 + rr * P:u * 256 + (rr + 1) * P],
                                words[:, c0:c0 + P],
                                ident[:],
                            )
                    st[("T", key, j, h)] = bank

        def exits(j):
            nr = ROW_TILES[j]
            gx = work.tile([P, nr * 512], BF16, name="gx%d" % j, tag="gx", align_bytes=64)
            ge = work.tile([P, nr * 512], BF16, name="ge%d" % j, tag="ge", bufs=3, align_bytes=64)
            st[("gx", j)] = gx
            st[("ge", j)] = ge
            plan = [("xn", gx, h) for h in range(nr // 2)] + [("en", ge, h) for h in range(nr // 2)]
            n_vec = vector_exits(j)
            for i, (key, dst, h) in enumerate(plan):
                src = st[("T", key, j, h)][:].rearrange("q (u c) -> q c u", u=2)
                d = dst[:].bitcast(F32)[:, h * 512:(h + 1) * 512].rearrange("q (c u) -> q c u", u=2)
                if i >= len(plan) - n_vec:
                    nc.vector.tensor_copy(out=d, in_=src)
                else:
                    nc.scalar.copy(out=d, in_=src)

        def quant(src, nm, j, bufs):
            cols = ROW_TILES[j] * P
            codes = work.tile([P, cols], U32, name="%sc%d" % (nm, j), tag=nm + "c", bufs=bufs, align_bytes=64)
            scales = work.tile([P, cols], U8, name="%ss%d" % (nm, j), tag=nm + "s", bufs=bufs, align_bytes=64)
            nc.vector.quantize_mx(out=codes[:].bitcast(FP8X4), scales=scales[:], in_=src[:])
            st[(nm, j)] = (codes, scales)

        def stage1(j):
            n = ROW_TILES[j] * P
            per_bank = 512 // n
            xc, xs = st[("x", j)]
            ec, es = st[("e", j)]
            bank = None
            for m in range(4):
                cols = slice(m * P, (m + 1) * P)
                if m % per_bank == 0:
                    bank = new_bank()
                acc = bank[:, (m % per_bank) * n:(m % per_bank + 1) * n]
                nc.tensor.matmul_mx(
                    out=acc, lhsT=wic[:, cols].bitcast(FP8X4), lhsT_scale=wis[:, cols],
                    rhs=xc[:].bitcast(FP8X4), rhs_scale=xs[:], start=True, stop=False,
                )
                nc.tensor.matmul_mx(
                    out=acc, lhsT=whc[:, cols].bitcast(FP8X4), lhsT_scale=whs[:, cols],
                    rhs=ec[:].bitcast(FP8X4), rhs_scale=es[:], start=False, stop=True,
                )
                st[("M", j, m)] = acc

        def sigmoid(j):
            n = ROW_TILES[j] * P
            sig = work.tile([P, 4 * n], F32, name="sig%d" % j, tag="sig")
            for m in range(4):
                nc.scalar.activation(
                    out=sig[:, m * n:(m + 1) * n], in_=st[("M", j, m)],
                    func=ACT.Sigmoid, bias=bias_f[:, m:m + 1], scale=1.0,
                )
            st[("sig", j)] = sig

        def mult(j):
            n = ROW_TILES[j] * P
            gg = work.tile([P, 4 * n], BF16, name="gg%d" % j, tag="gg", align_bytes=64)
            nv = n - gpsimd_cols(j)
            planes = st[("sig", j)][:].rearrange("p (t c) -> p t c", t=4)
            ge = st[("ge", j)]
            nc.vector.tensor_tensor(
                out=gg[:, :4 * nv].rearrange("p (c i t) -> p c t i", i=4, t=4),
                in0=planes[:, :, :nv].rearrange("p t (c i) -> p c t i", i=4),
                in1=ge[:, :4 * nv].rearrange("p (c i t) -> p c t i", i=4, t=4),
                op=ALU.mult,
            )
            if nv < n:
                nc.gpsimd.tensor_tensor(
                    out=gg[:, 4 * nv:].rearrange("p (c t) -> p c t", t=4),
                    in0=planes[:, :, nv:].rearrange("p t c -> p c t"),
                    in1=ge[:, 4 * nv:].rearrange("p (c t) -> p c t", t=4),
                    op=ALU.mult,
                )
            st[("gg", j)] = gg

        def stage2(j):
            gc, gs = st[("g", j)]
            wtc, wts = st["wt"]
            for h in range(ROW_TILES[j] // 2):
                bank = new_bank()
                for rr in range(2):
                    cols = slice((2 * h + rr) * P, (2 * h + rr + 1) * P)
                    nc.tensor.matmul_mx(
                        out=bank[:, rr * H:(rr + 1) * H],
                        lhsT=gc[:, cols].bitcast(FP8X4), lhsT_scale=gs[:, cols],
                        rhs=wtc[:].bitcast(FP8X4), rhs_scale=wts[:], start=True, stop=True,
                    )
                st[("O", j, h)] = bank

        def oexit_store(j):
            nr = ROW_TILES[j]
            osb = work.tile([P, nr * H], F32, name="osb%d" % j, tag="osb", bufs=3)
            for h in range(nr // 2):
                nc.scalar.copy(out=osb[:, h * 512:(h + 1) * 512], in_=st[("O", j, h)][:])
            nc.sync.dma_start(
                out=out[ROW0[j]:ROW0[j] + nr * P, :].rearrange("(p r) h -> p (r h)", r=nr), in_=osb[:]
            )

        for s in range(-2, NB + S2_LAG):
            while loaded[0] < NB and loaded[0] <= s + LOOKAHEAD:
                load(loaded[0])
                loaded[0] += 1
            if s + 2 < NB:
                transposes(s + 2)
            if 0 <= s < NB:
                mult(s)
            if s + 2 < NB:
                exits(s + 2)
            if s == 0:
                quant_wt()
            if 0 <= s + 1 < NB:
                stage1(s + 1)
                sigmoid(s + 1)
            if s + 2 < NB:
                quant(st[("gx", s + 2)], "x", s + 2, 2)
                quant(st[("ge", s + 2)], "e", s + 2, 2)
            if 0 <= s < NB:
                quant(st[("gg", s)], "g", s, 2 + S2_LAG)
            if s == -1:
                prep_wt()
            if 0 <= s - S2_LAG < NB:
                stage2(s - S2_LAG)
                oexit_store(s - S2_LAG)
